import numpy as np
import ml_dtypes


def mxq(x, axis, fmt="e4m3"):
    dtype, down = {"e4m3": (ml_dtypes.float8_e4m3fn, 7), "e5m2": (ml_dtypes.float8_e5m2, 14)}[fmt]
    v = np.moveaxis(np.asarray(x, np.float32).astype(ml_dtypes.bfloat16).astype(np.float64), axis, -1)
    blocks = v.reshape(v.shape[:-1] + (-1, 32))
    amax = np.abs(blocks).max(-1, keepdims=True)
    byte = np.maximum(np.where(amax > 0, np.frexp(amax)[1] - 1 + 127, 0) - down, 1)
    scale = np.exp2(byte - 127.0)
    codes = (blocks / scale).astype(np.float32).astype(dtype).astype(np.float64)
    return np.moveaxis((codes * scale).reshape(v.shape), -1, axis)


WIDE = False


def mx_kscale(k):
    if not WIDE:
        return np.ones(k)
    levels = np.array([10, -10, 5, -5, 0])
    a = np.random.permutation(np.resize(levels, k // 512 * 4)).reshape(k // 512, 4)
    idx = np.arange(k)
    return np.exp2(a[idx // 512, idx % 128 // 32])


BF16 = ml_dtypes.bfloat16


def bf(x):
    return np.asarray(x, np.float32).astype(BF16)


def f64(x):
    return np.asarray(x).astype(np.float64)


N, M, D, DV = 8192, 512, 1024, 256
EPS = 1e-12


def setup_inputs():
    s = mx_kscale(D)
    return {"q": bf(np.random.standard_normal((N, D)) * 0.6 * s),
            "k": bf(np.random.standard_normal((M, D)) * 0.6 / s),
            "v": bf(np.random.standard_normal((M, DV)) * 0.6)}


def reference(q, k, v):
    s = mxq(f64(q), 1, "e4m3") @ mxq(f64(k), 1, "e4m3").T
    norm = np.sqrt(np.sum(s * s, axis=1, keepdims=True))
    w = s / np.maximum(norm, EPS)
    return mxq(w, 1, "e4m3") @ mxq(f64(v), 0, "e4m3")

@@ -1,0 +1,276 @@
+from contextlib import ExitStack
+
+import concourse.mybir as mybir
+from concourse.masks import make_identity
+
+F32 = mybir.dt.float32
+BF16 = mybir.dt.bfloat16
+U32 = mybir.dt.uint32
+U8 = mybir.dt.uint8
+FP8X4 = mybir.dt.float8_e4m3fn_x4
+ACT = mybir.ActivationFunctionType
+ALU = mybir.AluOpType
+
+N_QUERIES, N_KEYS, D_FEAT, D_VAL = 8192, 512, 1024, 256
+EPS = 1e-12
+
+P = 128
+PACK = 4
+K_PASS = P * PACK
+FEAT_PASSES = D_FEAT // K_PASS
+KEY_TILES = N_KEYS // P
+Q_TILES = N_QUERIES // P
+PAIR = 2
+ROUNDS = Q_TILES // PAIR
+CHUNK = 4
+N_CHUNKS = Q_TILES // CHUNK
+BLOCKS = 4
+
+FLOPS = 2 * N_QUERIES * N_KEYS * (D_FEAT + D_VAL)
+
+
+def words_of(rows_bf16):
+    return rows_bf16.bitcast(F32)
+
+
+def transpose_blocks(nc, bank, blocks, ident):
+    for j, block in enumerate(blocks):
+        nc.tensor.transpose(bank[:, j, :], block, ident[:])
+
+
+def copy_interleaved(copy, grouped_words, bank):
+    copy(
+        out=grouped_words.rearrange("p (a r u) -> p a r u", a=2, u=2),
+        in_=bank[:].rearrange("p (a u) r -> p a r u", u=2),
+    )
+
+
+def tile_selfattention_pa_t_kernel(tc, q, k, v, out):
+    nc = tc.nc
+    q_rows = q.rearrange("(p n) d -> p n d", n=Q_TILES)
+    out_rows = out.rearrange("(p n) c -> p n c", n=Q_TILES)
+
+    with ExitStack() as ctx:
+        ctx.enter_context(tc.manual_schedule())
+
+        consts = ctx.enter_context(tc.tile_pool(name="consts", bufs=1))
+        q_pool = ctx.enter_context(tc.tile_pool(name="q_pool", bufs=N_CHUNKS))
+        work = ctx.enter_context(tc.tile_pool(name="work", bufs=3))
+        o_pool = ctx.enter_context(tc.tile_pool(name="o_pool", bufs=4))
+        ps_t = ctx.enter_context(tc.psum_pool(name="ps_t", bufs=PAIR))
+        ps_s = ctx.enter_context(tc.psum_pool(name="ps_s", bufs=2 * PAIR))
+        ps_w = ctx.enter_context(tc.psum_pool(name="ps_w", bufs=1))
+        ps_o = ctx.enter_context(tc.psum_pool(name="ps_o", bufs=1))
+
+        q_chunks = []
+
+        def load_chunk(ch):
+            q_chunk = q_pool.tile([P, CHUNK, D_FEAT], BF16)
+            nc.sync.dma_start(out=q_chunk[:], in_=q_rows[:, ch * CHUNK : (ch + 1) * CHUNK, :])
+            q_chunks.append(q_chunk)
+
+        k_sb = consts.tile([P, KEY_TILES, D_FEAT], BF16)
+        nc.sync.dma_start(out=k_sb[:], in_=k.rearrange("(a p) d -> p a d", p=P))
+        load_chunk(0)
+        v_raw = consts.tile([P, 2, 2 * D_VAL], BF16)
+        nc.sync.dma_start(out=v_raw[:], in_=v.rearrange("(u p e) c -> p u (e c)", u=2, e=2))
+        for ch in range(1, N_CHUNKS):
+            load_chunk(ch)
+
+        ident = consts.tile([P, P], F32)
+        make_identity(nc, ident[:])
+
+        one = consts.tile([P, 1], F32)
+        nc.vector.memset(one[:], 1.0)
+        table_warm = consts.tile([P, 1], F32)
+        nc.scalar.activation(out=table_warm[:], in_=one[:], func=ACT.Sqrt)
+
+        k_grp = consts.tile([P, FEAT_PASSES * N_KEYS * PACK], BF16, align_bytes=64)
+        k_codes = consts.tile([P, FEAT_PASSES, N_KEYS], U32, align_bytes=64)
+        k_scales = consts.tile([P, FEAT_PASSES, N_KEYS], U8, align_bytes=64)
+        for c in range(FEAT_PASSES):
+            for half in range(KEY_TILES // 2):
+                bank = ps_t.tile([P, BLOCKS, P], F32, name="t_bank")
+                blocks = [
+                    words_of(k_sb[:, 2 * half + a, :])[:, (2 * c + u) * P : (2 * c + u + 1) * P]
+                    for a in range(2)
+                    for u in range(2)
+                ]
+                transpose_blocks(nc, bank, blocks, ident)
+                first = (c * N_KEYS + half * 2 * P) * 2
+                copy = nc.scalar.copy if half == 0 else nc.vector.tensor_copy
+                copy_interleaved(copy, words_of(k_grp[:])[:, first : first + BLOCKS * P], bank)
+        for c in range(FEAT_PASSES):
+            nc.vector.quantize_mx(
+                out=k_codes[:, c, :].bitcast(FP8X4),
+                scales=k_scales[:, c, :],
+                in_=k_grp[:, c * N_KEYS * PACK : (c + 1) * N_KEYS * PACK],
+            )
+
+        t_banks, q_grps, q_codes, q_scales = {}, {}, {}, {}
+        s_banks, norms, w_rows = {}, {}, {}
+        w_banks, w_grps, w_codes, w_scales = {}, {}, {}, {}
+        o_banks, o_chunks = {}, {}
+
+        def transpose_queries(r):
+            for i in range(PAIR):
+                n = r * PAIR + i
+                row_words = words_of(q_chunks[n // CHUNK][:, n % CHUNK, :])
+                bank = ps_t.tile([P, BLOCKS, P], F32, name="t_bank")
+                blocks = [row_words[:, j * P : (j + 1) * P] for j in range(BLOCKS)]
+                transpose_blocks(nc, bank, blocks, ident)
+                t_banks[n] = bank
+
+        def group_queries(r):
+            q_grp = work.tile([P, PAIR * D_FEAT], BF16, align_bytes=64)
+            for i in range(PAIR):
+                tile_words = words_of(q_grp[:])[:, i * BLOCKS * P : (i + 1) * BLOCKS * P]
+                copy_interleaved(nc.scalar.copy, tile_words, t_banks[r * PAIR + i])
+            q_grps[r] = q_grp
+
+        def quantise_queries(r):
+            q_code = work.tile([P, PAIR * FEAT_PASSES * P], U32, align_bytes=64)
+            q_scale = work.tile([P, PAIR * FEAT_PASSES * P], U8, align_bytes=64)
+            nc.vector.quantize_mx(out=q_code[:].bitcast(FP8X4), scales=q_scale[:], in_=q_grps[r][:])
+            q_codes[r], q_scales[r] = q_code, q_scale
+
+        def scores(r):
+            for i in range(PAIR):
+                s_bank = ps_s.tile([P, N_KEYS], F32)
+                for c in range(FEAT_PASSES):
+                    cols = slice((i * FEAT_PASSES + c) * P, (i * FEAT_PASSES + c + 1) * P)
+                    nc.tensor.matmul_mx(
+                        out=s_bank[:],
+                        lhsT=q_codes[r][:, cols].bitcast(FP8X4),
+                        lhsT_scale=q_scales[r][:, cols],
+                        rhs=k_codes[:, c, :].bitcast(FP8X4),
+                        rhs_scale=k_scales[:, c, :],
+                        start=(c == 0),
+                        stop=(c == FEAT_PASSES - 1),
+                    )
+                s_banks[r * PAIR + i] = s_bank
+
+        def row_norms(r):
+            sumsq = work.tile([P, PAIR], F32)
+            for i in range(PAIR):
+                squares = work.tile([P, N_KEYS], BF16)
+                nc.scalar.activation(
+                    out=squares[:],
+                    in_=s_banks[r * PAIR + i][:],
+                    func=ACT.Square,
+                    accum_out=sumsq[:, i : i + 1],
+                )
+            norm = work.tile([P, PAIR], F32)
+            nc.scalar.activation(out=norm[:], in_=sumsq[:], func=ACT.Sqrt)
+            norms[r] = norm
+
+        def normalise(r):
+            floored = work.tile([P, PAIR], F32)
+            nc.vector.tensor_scalar(
+                out=floored[:], in0=norms[r][:], scalar1=EPS, scalar2=None, op0=ALU.max
+            )
+            inverse = work.tile([P, PAIR], F32)
+            nc.vector.reciprocal(out=inverse[:], in_=floored[:])
+            w_row = work.tile([P, PAIR, N_KEYS], BF16)
+            for i in range(PAIR):
+                nc.vector.tensor_scalar(
+                    out=w_row[:, i, :],
+                    in0=s_banks[r * PAIR + i][:],
+                    scalar1=inverse[:, i : i + 1],
+                    scalar2=None,
+                    op0=ALU.mult,
+                )
+            w_rows[r] = w_row
+
+        def transpose_weights(r):
+            w_bank = ps_w.tile([P, BLOCKS, P], F32)
+            blocks = [
+                words_of(w_rows[r][:, i, :])[:, u * P : (u + 1) * P]
+                for i in range(PAIR)
+                for u in range(2)
+            ]
+            transpose_blocks(nc, w_bank, blocks, ident)
+            w_banks[r] = w_bank
+
+        def group_weights(r):
+            w_grp = work.tile([P, PAIR * N_KEYS], BF16, align_bytes=64)
+            copy_interleaved(nc.vector.tensor_copy, words_of(w_grp[:]), w_banks[r])
+            w_grps[r] = w_grp
+
+        def quantise_weights(r):
+            w_code = work.tile([P, PAIR * P], U32, align_bytes=64)
+            w_scale = work.tile([P, PAIR * P], U8, align_bytes=64)
+            nc.vector.quantize_mx(out=w_code[:].bitcast(FP8X4), scales=w_scale[:], in_=w_grps[r][:])
+            w_codes[r], w_scales[r] = w_code, w_scale
+
+        def attend(r):
+            o_bank = ps_o.tile([P, PAIR, D_VAL], F32)
+            for i in range(PAIR):
+                cols = slice(i * P, (i + 1) * P)
+                nc.tensor.matmul_mx(
+                    out=o_bank[:, i, :],
+                    lhsT=w_codes[r][:, cols].bitcast(FP8X4),
+                    lhsT_scale=w_scales[r][:, cols],
+                    rhs=v_codes[:].bitcast(FP8X4),
+                    rhs_scale=v_scales[:],
+                    start=True,
+                    stop=True,
+                )
+            o_banks[r] = o_bank
+
+        def leave(r):
+            ch, half = divmod(r, CHUNK // PAIR)
+            if half == 0:
+                o_chunks[ch] = o_pool.tile([P, CHUNK, D_VAL], F32, name="o_chunk")
+            copy = nc.scalar.copy if r % 2 == 0 else nc.vector.tensor_copy
+            copy(out=o_chunks[ch][:, half * PAIR : (half + 1) * PAIR, :], in_=o_banks[r][:])
+            if half == CHUNK // PAIR - 1:
+                nc.sync.dma_start(
+                    out=out_rows[:, ch * CHUNK : (ch + 1) * CHUNK, :], in_=o_chunks[ch][:]
+                )
+
+        transpose_queries(0)
+        group_queries(0)
+        quantise_queries(0)
+
+        v_grp = consts.tile([P, D_VAL, PACK], BF16, align_bytes=64)
+        v_codes = consts.tile([P, D_VAL], U32, align_bytes=64)
+        v_scales = consts.tile([P, D_VAL], U8, align_bytes=64)
+        nc.vector.tensor_copy(
+            out=v_grp[:].rearrange("p c (u e) -> p c u e", e=2),
+            in_=v_raw[:].rearrange("p u (e c) -> p c u e", e=2),
+        )
+        nc.vector.quantize_mx(
+            out=v_codes[:].bitcast(FP8X4),
+            scales=v_scales[:],
+            in_=v_grp[:].rearrange("p c t -> p (c t)"),
+        )
+
+        def live(r):
+            return 0 <= r < ROUNDS
+
+        for r in range(ROUNDS + 3):
+            if live(r + 1):
+                transpose_queries(r + 1)
+            if live(r - 2):
+                transpose_weights(r - 2)
+            if live(r):
+                scores(r)
+            if live(r - 3):
+                attend(r - 3)
+
+            if live(r + 1):
+                group_queries(r + 1)
+            if live(r):
+                row_norms(r)
+
+            if live(r - 1):
+                normalise(r - 1)
+            if live(r - 2):
+                group_weights(r - 2)
+            if live(r + 1):
+                quantise_queries(r + 1)
+            if live(r - 2):
+                quantise_weights(r - 2)
+            if live(r - 3):
+                leave(r - 3)

@@ -108,7 +108,7 @@ def tile_selfattention_pa_t_kernel(tc, q, k, v, out):
             )
 
         t_banks, q_grps, q_codes, q_scales = {}, {}, {}, {}
-        s_banks, norms, w_rows = {}, {}, {}
+        s_banks, sumsqs, norms, floors, inverses, w_rows = {}, {}, {}, {}, {}, {}
         w_banks, w_grps, w_codes, w_scales = {}, {}, {}, {}
         o_banks, o_chunks = {}, {}
 
@@ -150,7 +150,7 @@ def tile_selfattention_pa_t_kernel(tc, q, k, v, out):
                     )
                 s_banks[r * PAIR + i] = s_bank
 
-        def row_norms(r):
+        def square_sums(r):
             sumsq = work.tile([P, PAIR], F32)
             for i in range(PAIR):
                 squares = work.tile([P, N_KEYS], BF16)
@@ -160,23 +160,32 @@ def tile_selfattention_pa_t_kernel(tc, q, k, v, out):
                     func=ACT.Square,
                     accum_out=sumsq[:, i : i + 1],
                 )
+            sumsqs[r] = sumsq
+
+        def root(r):
             norm = work.tile([P, PAIR], F32)
-            nc.scalar.activation(out=norm[:], in_=sumsq[:], func=ACT.Sqrt)
+            nc.scalar.activation(out=norm[:], in_=sumsqs[r][:], func=ACT.Sqrt)
             norms[r] = norm
 
-        def normalise(r):
+        def floor_norm(r):
             floored = work.tile([P, PAIR], F32)
             nc.vector.tensor_scalar(
                 out=floored[:], in0=norms[r][:], scalar1=EPS, scalar2=None, op0=ALU.max
             )
+            floors[r] = floored
+
+        def invert_norm(r):
             inverse = work.tile([P, PAIR], F32)
-            nc.vector.reciprocal(out=inverse[:], in_=floored[:])
+            nc.vector.reciprocal(out=inverse[:], in_=floors[r][:])
+            inverses[r] = inverse
+
+        def scale_scores(r):
             w_row = work.tile([P, PAIR, N_KEYS], BF16)
             for i in range(PAIR):
                 nc.vector.tensor_scalar(
                     out=w_row[:, i, :],
                     in0=s_banks[r * PAIR + i][:],
-                    scalar1=inverse[:, i : i + 1],
+                    scalar1=inverses[r][:, i : i + 1],
                     scalar2=None,
                     op0=ALU.mult,
                 )
@@ -222,8 +231,9 @@ def tile_selfattention_pa_t_kernel(tc, q, k, v, out):
             ch, half = divmod(r, CHUNK // PAIR)
             if half == 0:
                 o_chunks[ch] = o_pool.tile([P, CHUNK, D_VAL], F32, name="o_chunk")
-            copy = nc.scalar.copy if r % 2 == 0 else nc.vector.tensor_copy
-            copy(out=o_chunks[ch][:, half * PAIR : (half + 1) * PAIR, :], in_=o_banks[r][:])
+            nc.scalar.copy(
+                out=o_chunks[ch][:, half * PAIR : (half + 1) * PAIR, :], in_=o_banks[r][:]
+            )
             if half == CHUNK // PAIR - 1:
                 nc.sync.dma_start(
                     out=out_rows[:, ch * CHUNK : (ch + 1) * CHUNK, :], in_=o_chunks[ch][:]
@@ -231,6 +241,8 @@ def tile_selfattention_pa_t_kernel(tc, q, k, v, out):
 
         transpose_queries(0)
         group_queries(0)
+        transpose_queries(1)
+        group_queries(1)
         quantise_queries(0)
 
         v_grp = consts.tile([P, D_VAL, PACK], BF16, align_bytes=64)
@@ -249,28 +261,34 @@ def tile_selfattention_pa_t_kernel(tc, q, k, v, out):
         def live(r):
             return 0 <= r < ROUNDS
 
-        for r in range(ROUNDS + 3):
-            if live(r + 1):
-                transpose_queries(r + 1)
-            if live(r - 2):
-                transpose_weights(r - 2)
+        for r in range(ROUNDS + 4):
+            if live(r + 2):
+                transpose_queries(r + 2)
+            if live(r - 3):
+                transpose_weights(r - 3)
             if live(r):
                 scores(r)
-            if live(r - 3):
-                attend(r - 3)
+            if live(r - 4):
+                attend(r - 4)
 
-            if live(r + 1):
-                group_queries(r + 1)
+            if live(r + 2):
+                group_queries(r + 2)
             if live(r):
-                row_norms(r)
+                square_sums(r)
+            if live(r - 4):
+                leave(r - 4)
+            if live(r):
+                root(r)
 
             if live(r - 1):
-                normalise(r - 1)
-            if live(r - 2):
-                group_weights(r - 2)
+                floor_norm(r - 1)
+            if live(r - 3):
+                group_weights(r - 3)
+            if live(r - 1):
+                invert_norm(r - 1)
             if live(r + 1):
                 quantise_queries(r + 1)
-            if live(r - 2):
-                quantise_weights(r - 2)
+            if live(r - 1):
+                scale_scores(r - 1)
             if live(r - 3):
-                leave(r - 3)
+                quantise_weights(r - 3)

@@ -22,8 +22,6 @@ KEY_TILES = N_KEYS // P
 Q_TILES = N_QUERIES // P
 PAIR = 2
 ROUNDS = Q_TILES // PAIR
-CHUNK = 4
-N_CHUNKS = Q_TILES // CHUNK
 BLOCKS = 4
 
 FLOPS = 2 * N_QUERIES * N_KEYS * (D_FEAT + D_VAL)
@@ -54,45 +52,48 @@ def tile_selfattention_pa_t_kernel(tc, q, k, v, out):
         ctx.enter_context(tc.manual_schedule())
 
         consts = ctx.enter_context(tc.tile_pool(name="consts", bufs=1))
-        q_pool = ctx.enter_context(tc.tile_pool(name="q_pool", bufs=N_CHUNKS))
+        q_pool = ctx.enter_context(tc.tile_pool(name="q_pool", bufs=ROUNDS))
         work = ctx.enter_context(tc.tile_pool(name="work", bufs=3))
-        o_pool = ctx.enter_context(tc.tile_pool(name="o_pool", bufs=4))
+        o_pool = ctx.enter_context(tc.tile_pool(name="o_pool", bufs=8))
         ps_t = ctx.enter_context(tc.psum_pool(name="ps_t", bufs=PAIR))
         ps_s = ctx.enter_context(tc.psum_pool(name="ps_s", bufs=2 * PAIR))
         ps_w = ctx.enter_context(tc.psum_pool(name="ps_w", bufs=1))
         ps_o = ctx.enter_context(tc.psum_pool(name="ps_o", bufs=1))
 
-        q_chunks = []
+        q_pairs = []
 
-        def load_chunk(ch):
-            q_chunk = q_pool.tile([P, CHUNK, D_FEAT], BF16)
-            nc.sync.dma_start(out=q_chunk[:], in_=q_rows[:, ch * CHUNK : (ch + 1) * CHUNK, :])
-            q_chunks.append(q_chunk)
+        def load_pair(r):
+            q_pair = q_pool.tile([P, PAIR, D_FEAT], BF16)
+            nc.sync.dma_start(out=q_pair[:], in_=q_rows[:, r * PAIR : (r + 1) * PAIR, :])
+            q_pairs.append(q_pair)
 
-        k_sb = consts.tile([P, KEY_TILES, D_FEAT], BF16)
-        nc.sync.dma_start(out=k_sb[:], in_=k.rearrange("(a p) d -> p a d", p=P))
-        load_chunk(0)
+        k_tiled = k.rearrange("(a p) d -> p a d", p=P)
+        k_rows = []
+        for c in range(FEAT_PASSES):
+            k_pass = consts.tile([P, KEY_TILES, K_PASS], BF16, name="k_pass%d" % c)
+            nc.sync.dma_start(out=k_pass[:], in_=k_tiled[:, :, c * K_PASS : (c + 1) * K_PASS])
+            k_rows.append(k_pass)
+        load_pair(0)
+        load_pair(1)
         v_raw = consts.tile([P, 2, 2 * D_VAL], BF16)
         nc.sync.dma_start(out=v_raw[:], in_=v.rearrange("(u p e) c -> p u (e c)", u=2, e=2))
-        for ch in range(1, N_CHUNKS):
-            load_chunk(ch)
+        for r in range(2, ROUNDS):
+            load_pair(r)
 
         ident = consts.tile([P, P], F32)
         make_identity(nc, ident[:])
 
-        one = consts.tile([P, 1], F32)
-        nc.vector.memset(one[:], 1.0)
-        table_warm = consts.tile([P, 1], F32)
-        nc.scalar.activation(out=table_warm[:], in_=one[:], func=ACT.Sqrt)
+        minus_half = consts.tile([P, PAIR], F32)
+        nc.vector.memset(minus_half[:], -0.5)
 
         k_grp = consts.tile([P, FEAT_PASSES * N_KEYS * PACK], BF16, align_bytes=64)
         k_codes = consts.tile([P, FEAT_PASSES, N_KEYS], U32, align_bytes=64)
         k_scales = consts.tile([P, FEAT_PASSES, N_KEYS], U8, align_bytes=64)
         for c in range(FEAT_PASSES):
             for half in range(KEY_TILES // 2):
-                bank = ps_t.tile([P, BLOCKS, P], F32, name="t_bank")
+                bank = ps_s.tile([P, BLOCKS, P], F32, name="s_bank")
                 blocks = [
-                    words_of(k_sb[:, 2 * half + a, :])[:, (2 * c + u) * P : (2 * c + u + 1) * P]
+                    words_of(k_rows[c][:, 2 * half + a, :])[:, u * P : (u + 1) * P]
                     for a in range(2)
                     for u in range(2)
                 ]
@@ -108,14 +109,14 @@ def tile_selfattention_pa_t_kernel(tc, q, k, v, out):
             )
 
         t_banks, q_grps, q_codes, q_scales = {}, {}, {}, {}
-        s_banks, sumsqs, norms, floors, inverses, w_rows = {}, {}, {}, {}, {}, {}
+        s_banks, sumsqs, inverses, w_rows = {}, {}, {}, {}
         w_banks, w_grps, w_codes, w_scales = {}, {}, {}, {}
-        o_banks, o_chunks = {}, {}
+        o_banks = {}
 
         def transpose_queries(r):
             for i in range(PAIR):
                 n = r * PAIR + i
-                row_words = words_of(q_chunks[n // CHUNK][:, n % CHUNK, :])
+                row_words = words_of(q_pairs[r][:, i, :])
                 bank = ps_t.tile([P, BLOCKS, P], F32, name="t_bank")
                 blocks = [row_words[:, j * P : (j + 1) * P] for j in range(BLOCKS)]
                 transpose_blocks(nc, bank, blocks, ident)
@@ -162,21 +163,13 @@ def tile_selfattention_pa_t_kernel(tc, q, k, v, out):
                 )
             sumsqs[r] = sumsq
 
-        def root(r):
-            norm = work.tile([P, PAIR], F32)
-            nc.scalar.activation(out=norm[:], in_=sumsqs[r][:], func=ACT.Sqrt)
-            norms[r] = norm
-
-        def floor_norm(r):
+        def inverse_norms(r):
             floored = work.tile([P, PAIR], F32)
-            nc.vector.tensor_scalar(
-                out=floored[:], in0=norms[r][:], scalar1=EPS, scalar2=None, op0=ALU.max
+            nc.gpsimd.tensor_scalar(
+                out=floored[:], in0=sumsqs[r][:], scalar1=EPS * EPS, scalar2=None, op0=ALU.max
             )
-            floors[r] = floored
-
-        def invert_norm(r):
             inverse = work.tile([P, PAIR], F32)
-            nc.vector.reciprocal(out=inverse[:], in_=floors[r][:])
+            nc.gpsimd.tensor_tensor(out=inverse[:], in0=floored[:], in1=minus_half[:], op=ALU.pow)
             inverses[r] = inverse
 
         def scale_scores(r):
@@ -228,16 +221,9 @@ def tile_selfattention_pa_t_kernel(tc, q, k, v, out):
             o_banks[r] = o_bank
 
         def leave(r):
-            ch, half = divmod(r, CHUNK // PAIR)
-            if half == 0:
-                o_chunks[ch] = o_pool.tile([P, CHUNK, D_VAL], F32, name="o_chunk")
-            nc.scalar.copy(
-                out=o_chunks[ch][:, half * PAIR : (half + 1) * PAIR, :], in_=o_banks[r][:]
-            )
-            if half == CHUNK // PAIR - 1:
-                nc.sync.dma_start(
-                    out=out_rows[:, ch * CHUNK : (ch + 1) * CHUNK, :], in_=o_chunks[ch][:]
-                )
+            o_pair = o_pool.tile([P, PAIR, D_VAL], F32)
+            nc.scalar.copy(out=o_pair[:], in_=o_banks[r][:])
+            nc.sync.dma_start(out=out_rows[:, r * PAIR : (r + 1) * PAIR, :], in_=o_pair[:])
 
         transpose_queries(0)
         group_queries(0)
@@ -277,17 +263,14 @@ def tile_selfattention_pa_t_kernel(tc, q, k, v, out):
                 square_sums(r)
             if live(r - 4):
                 leave(r - 4)
-            if live(r):
-                root(r)
 
-            if live(r - 1):
-                floor_norm(r - 1)
-            if live(r - 3):
-                group_weights(r - 3)
-            if live(r - 1):
-                invert_norm(r - 1)
+            if live(r):
+                inverse_norms(r)
+
             if live(r + 1):
                 quantise_queries(r + 1)
+            if live(r - 3):
+                group_weights(r - 3)
             if live(r - 1):
                 scale_scores(r - 1)
             if live(r - 3):

@@ -22,6 +22,8 @@ KEY_TILES = N_KEYS // P
 Q_TILES = N_QUERIES // P
 PAIR = 2
 ROUNDS = Q_TILES // PAIR
+DRAIN = ROUNDS - PAIR
+VECTOR_LEAVE_EVERY = 4
 BLOCKS = 4
 
 FLOPS = 2 * N_QUERIES * N_KEYS * (D_FEAT + D_VAL)
@@ -55,10 +57,10 @@ def tile_selfattention_pa_t_kernel(tc, q, k, v, out):
         q_pool = ctx.enter_context(tc.tile_pool(name="q_pool", bufs=ROUNDS))
         work = ctx.enter_context(tc.tile_pool(name="work", bufs=3))
         o_pool = ctx.enter_context(tc.tile_pool(name="o_pool", bufs=8))
-        ps_t = ctx.enter_context(tc.psum_pool(name="ps_t", bufs=PAIR))
-        ps_s = ctx.enter_context(tc.psum_pool(name="ps_s", bufs=2 * PAIR))
-        ps_w = ctx.enter_context(tc.psum_pool(name="ps_w", bufs=1))
-        ps_o = ctx.enter_context(tc.psum_pool(name="ps_o", bufs=1))
+        psum = ctx.enter_context(tc.psum_pool(name="psum", bufs=1))
+
+        def psum_bank(tag, shape):
+            return psum.tile(shape, F32, name="bank_" + tag)
 
         q_pairs = []
 
@@ -69,10 +71,10 @@ def tile_selfattention_pa_t_kernel(tc, q, k, v, out):
 
         k_tiled = k.rearrange("(a p) d -> p a d", p=P)
         k_rows = []
-        for c in range(FEAT_PASSES):
-            k_pass = consts.tile([P, KEY_TILES, K_PASS], BF16, name="k_pass%d" % c)
-            nc.sync.dma_start(out=k_pass[:], in_=k_tiled[:, :, c * K_PASS : (c + 1) * K_PASS])
-            k_rows.append(k_pass)
+        for a in range(KEY_TILES):
+            k_row = consts.tile([P, D_FEAT], BF16, name="k_row%d" % a)
+            nc.sync.dma_start(out=k_row[:], in_=k_tiled[:, a, :])
+            k_rows.append(k_row)
         load_pair(0)
         load_pair(1)
         v_raw = consts.tile([P, 2, 2 * D_VAL], BF16)
@@ -89,24 +91,25 @@ def tile_selfattention_pa_t_kernel(tc, q, k, v, out):
         k_grp = consts.tile([P, FEAT_PASSES * N_KEYS * PACK], BF16, align_bytes=64)
         k_codes = consts.tile([P, FEAT_PASSES, N_KEYS], U32, align_bytes=64)
         k_scales = consts.tile([P, FEAT_PASSES, N_KEYS], U8, align_bytes=64)
-        for c in range(FEAT_PASSES):
-            for half in range(KEY_TILES // 2):
-                bank = ps_s.tile([P, BLOCKS, P], F32, name="s_bank")
-                blocks = [
-                    words_of(k_rows[c][:, 2 * half + a, :])[:, u * P : (u + 1) * P]
-                    for a in range(2)
-                    for u in range(2)
-                ]
-                transpose_blocks(nc, bank, blocks, ident)
-                first = (c * N_KEYS + half * 2 * P) * 2
-                copy = nc.scalar.copy if half == 0 else nc.vector.tensor_copy
-                copy_interleaved(copy, words_of(k_grp[:])[:, first : first + BLOCKS * P], bank)
-        for c in range(FEAT_PASSES):
-            nc.vector.quantize_mx(
-                out=k_codes[:, c, :].bitcast(FP8X4),
-                scales=k_scales[:, c, :],
-                in_=k_grp[:, c * N_KEYS * PACK : (c + 1) * N_KEYS * PACK],
+        k_words = words_of(k_grp[:]).rearrange("p (c k u) -> p c k u", c=FEAT_PASSES, u=2)
+        for a in range(KEY_TILES):
+            bank = psum_bank("s%d" % a, [P, BLOCKS, P])
+            blocks = [words_of(k_rows[a][:])[:, j * P : (j + 1) * P] for j in range(BLOCKS)]
+            transpose_blocks(nc, bank, blocks, ident)
+            copy = nc.scalar.copy if a % 2 == 0 else nc.vector.tensor_copy
+            copy(
+                out=k_words[:, :, a * P : (a + 1) * P, :],
+                in_=bank[:].rearrange("p (c u) r -> p c r u", u=2),
             )
+        for half in range(2):
+            for c in range(FEAT_PASSES):
+                keys = slice(half * 2 * P, (half + 1) * 2 * P)
+                first = (c * N_KEYS + half * 2 * P) * PACK
+                nc.vector.quantize_mx(
+                    out=k_codes[:, c, keys].bitcast(FP8X4),
+                    scales=k_scales[:, c, keys],
+                    in_=k_grp[:, first : first + 2 * P * PACK],
+                )
 
         t_banks, q_grps, q_codes, q_scales = {}, {}, {}, {}
         s_banks, sumsqs, inverses, w_rows = {}, {}, {}, {}
@@ -117,7 +120,7 @@ def tile_selfattention_pa_t_kernel(tc, q, k, v, out):
             for i in range(PAIR):
                 n = r * PAIR + i
                 row_words = words_of(q_pairs[r][:, i, :])
-                bank = ps_t.tile([P, BLOCKS, P], F32, name="t_bank")
+                bank = psum_bank(("w", "o")[i] if r == 1 else "t%d" % i, [P, BLOCKS, P])
                 blocks = [row_words[:, j * P : (j + 1) * P] for j in range(BLOCKS)]
                 transpose_blocks(nc, bank, blocks, ident)
                 t_banks[n] = bank
@@ -137,7 +140,7 @@ def tile_selfattention_pa_t_kernel(tc, q, k, v, out):
 
         def scores(r):
             for i in range(PAIR):
-                s_bank = ps_s.tile([P, N_KEYS], F32)
+                s_bank = psum_bank("s%d" % ((r * PAIR + i) % 4), [P, N_KEYS])
                 for c in range(FEAT_PASSES):
                     cols = slice((i * FEAT_PASSES + c) * P, (i * FEAT_PASSES + c + 1) * P)
                     nc.tensor.matmul_mx(
@@ -172,20 +175,20 @@ def tile_selfattention_pa_t_kernel(tc, q, k, v, out):
             nc.gpsimd.tensor_tensor(out=inverse[:], in0=floored[:], in1=minus_half[:], op=ALU.pow)
             inverses[r] = inverse
 
-        def scale_scores(r):
-            w_row = work.tile([P, PAIR, N_KEYS], BF16)
-            for i in range(PAIR):
+        def scale_scores(r, i, on_scalar=False):
+            if i == 0:
+                w_rows[r] = work.tile([P, PAIR, N_KEYS], BF16, name="w_row")
+            w_row, s_bank = w_rows[r][:, i, :], s_banks[r * PAIR + i][:]
+            inverse = inverses[r][:, i : i + 1]
+            if on_scalar:
+                nc.scalar.activation(out=w_row, in_=s_bank, func=ACT.Copy, scale=inverse)
+            else:
                 nc.vector.tensor_scalar(
-                    out=w_row[:, i, :],
-                    in0=s_banks[r * PAIR + i][:],
-                    scalar1=inverses[r][:, i : i + 1],
-                    scalar2=None,
-                    op0=ALU.mult,
+                    out=w_row, in0=s_bank, scalar1=inverse, scalar2=None, op0=ALU.mult
                 )
-            w_rows[r] = w_row
 
         def transpose_weights(r):
-            w_bank = ps_w.tile([P, BLOCKS, P], F32)
+            w_bank = psum_bank("w" if r < DRAIN - 3 else ("t0", "t1", "w")[r % 3], [P, BLOCKS, P])
             blocks = [
                 words_of(w_rows[r][:, i, :])[:, u * P : (u + 1) * P]
                 for i in range(PAIR)
@@ -194,9 +197,9 @@ def tile_selfattention_pa_t_kernel(tc, q, k, v, out):
             transpose_blocks(nc, w_bank, blocks, ident)
             w_banks[r] = w_bank
 
-        def group_weights(r):
+        def group_weights(r, copy):
             w_grp = work.tile([P, PAIR * N_KEYS], BF16, align_bytes=64)
-            copy_interleaved(nc.vector.tensor_copy, words_of(w_grp[:]), w_banks[r])
+            copy_interleaved(copy, words_of(w_grp[:]), w_banks[r])
             w_grps[r] = w_grp
 
         def quantise_weights(r):
@@ -206,7 +209,7 @@ def tile_selfattention_pa_t_kernel(tc, q, k, v, out):
             w_codes[r], w_scales[r] = w_code, w_scale
 
         def attend(r):
-            o_bank = ps_o.tile([P, PAIR, D_VAL], F32)
+            o_bank = psum_bank("o" if r < DRAIN - 2 else ("o", "s0", "s1")[r % 3], [P, PAIR, D_VAL])
             for i in range(PAIR):
                 cols = slice(i * P, (i + 1) * P)
                 nc.tensor.matmul_mx(
@@ -220,34 +223,32 @@ def tile_selfattention_pa_t_kernel(tc, q, k, v, out):
                 )
             o_banks[r] = o_bank
 
+        def leaves_on_vector(r):
+            return r % VECTOR_LEAVE_EVERY == 0 and r < DRAIN - 2
+
         def leave(r):
             o_pair = o_pool.tile([P, PAIR, D_VAL], F32)
-            nc.scalar.copy(out=o_pair[:], in_=o_banks[r][:])
+            copy = nc.vector.tensor_copy if leaves_on_vector(r) else nc.scalar.copy
+            copy(out=o_pair[:], in_=o_banks[r][:])
             nc.sync.dma_start(out=out_rows[:, r * PAIR : (r + 1) * PAIR, :], in_=o_pair[:])
 
         transpose_queries(0)
-        group_queries(0)
         transpose_queries(1)
+        group_queries(0)
         group_queries(1)
         quantise_queries(0)
 
-        v_grp = consts.tile([P, D_VAL, PACK], BF16, align_bytes=64)
         v_codes = consts.tile([P, D_VAL], U32, align_bytes=64)
         v_scales = consts.tile([P, D_VAL], U8, align_bytes=64)
-        nc.vector.tensor_copy(
-            out=v_grp[:].rearrange("p c (u e) -> p c u e", e=2),
-            in_=v_raw[:].rearrange("p u (e c) -> p c u e", e=2),
-        )
-        nc.vector.quantize_mx(
-            out=v_codes[:].bitcast(FP8X4),
-            scales=v_scales[:],
-            in_=v_grp[:].rearrange("p c t -> p (c t)"),
-        )
+        v_grp = consts.tile([P, D_VAL, PACK], BF16, align_bytes=64)
 
         def live(r):
             return 0 <= r < ROUNDS
 
         for r in range(ROUNDS + 4):
+            if live(r - 5) and leaves_on_vector(r - 5):
+                leave(r - 5)
+
             if live(r + 2):
                 transpose_queries(r + 2)
             if live(r - 3):
@@ -259,9 +260,13 @@ def tile_selfattention_pa_t_kernel(tc, q, k, v, out):
 
             if live(r + 2):
                 group_queries(r + 2)
+            if r == DRAIN:
+                group_weights(r - 3, nc.scalar.copy)
             if live(r):
                 square_sums(r)
-            if live(r - 4):
+            if r == ROUNDS:
+                scale_scores(r - 1, 0, on_scalar=True)
+            if live(r - 4) and not leaves_on_vector(r - 4):
                 leave(r - 4)
 
             if live(r):
@@ -269,9 +274,20 @@ def tile_selfattention_pa_t_kernel(tc, q, k, v, out):
 
             if live(r + 1):
                 quantise_queries(r + 1)
-            if live(r - 3):
-                group_weights(r - 3)
+            if live(r - 3) and r != DRAIN:
+                group_weights(r - 3, nc.vector.tensor_copy)
             if live(r - 1):
-                scale_scores(r - 1)
+                for i in range(PAIR) if r < ROUNDS else (1,):
+                    scale_scores(r - 1, i)
+            if r == 1:
+                nc.vector.tensor_copy(
+                    out=v_grp[:].rearrange("p c (u e) -> p c u e", e=2),
+                    in_=v_raw[:].rearrange("p u (e c) -> p c u e", e=2),
+                )
+                nc.vector.quantize_mx(
+                    out=v_codes[:].bitcast(FP8X4),
+                    scales=v_scales[:],
+                    in_=v_grp[:].rearrange("p c t -> p (c t)"),
+                )
             if live(r - 3):
                 quantise_weights(r - 3)

@@ -24,6 +24,7 @@ PAIR = 2
 ROUNDS = Q_TILES // PAIR
 DRAIN = ROUNDS - PAIR
 VECTOR_LEAVE_EVERY = 4
+LAST = ROUNDS - 1
 BLOCKS = 4
 
 FLOPS = 2 * N_QUERIES * N_KEYS * (D_FEAT + D_VAL)
@@ -40,8 +41,8 @@ def transpose_blocks(nc, bank, blocks, ident):
 
 def copy_interleaved(copy, grouped_words, bank):
     copy(
-        out=grouped_words.rearrange("p (a r u) -> p a r u", a=2, u=2),
-        in_=bank[:].rearrange("p (a u) r -> p a r u", u=2),
+        out=grouped_words.rearrange("p (a r u) -> p a r u", r=P, u=2),
+        in_=bank.rearrange("p (a u) r -> p a r u", u=2),
     )
 
 
@@ -62,12 +63,17 @@ def tile_selfattention_pa_t_kernel(tc, q, k, v, out):
         def psum_bank(tag, shape):
             return psum.tile(shape, F32, name="bank_" + tag)
 
-        q_pairs = []
+        q_tiles = []
 
-        def load_pair(r):
+        def load_pair(r, loads=1):
             q_pair = q_pool.tile([P, PAIR, D_FEAT], BF16)
-            nc.sync.dma_start(out=q_pair[:], in_=q_rows[:, r * PAIR : (r + 1) * PAIR, :])
-            q_pairs.append(q_pair)
+            size = PAIR // loads
+            for i in range(0, PAIR, size):
+                first = r * PAIR + i
+                nc.sync.dma_start(
+                    out=q_pair[:, i : i + size, :], in_=q_rows[:, first : first + size, :]
+                )
+            q_tiles.extend([q_pair[:, i, :] for i in range(PAIR)])
 
         k_tiled = k.rearrange("(a p) d -> p a d", p=P)
         k_rows = []
@@ -75,12 +81,29 @@ def tile_selfattention_pa_t_kernel(tc, q, k, v, out):
             k_row = consts.tile([P, D_FEAT], BF16, name="k_row%d" % a)
             nc.sync.dma_start(out=k_row[:], in_=k_tiled[:, a, :])
             k_rows.append(k_row)
-        load_pair(0)
+        load_pair(0, loads=PAIR)
         load_pair(1)
+        load_pair(2)
         v_raw = consts.tile([P, 2, 2 * D_VAL], BF16)
         nc.sync.dma_start(out=v_raw[:], in_=v.rearrange("(u p e) c -> p u (e c)", u=2, e=2))
-        for r in range(2, ROUNDS):
+        for r in range(3, ROUNDS):
             load_pair(r)
+
+        zeros = consts.tile([P, N_KEYS], BF16)
+        nc.vector.memset(zeros[:], 0.0)
+
+        def stay_warm(columns, tag):
+            bank = psum_bank(tag, [P, N_KEYS])
+            nc.tensor.matmul(
+                out=bank[:, :columns],
+                lhsT=zeros[:, :P],
+                rhs=zeros[:, :columns],
+                start=True,
+                stop=True,
+            )
+
+        for step in range(4):
+            stay_warm(N_KEYS, "o")
 
         ident = consts.tile([P, P], F32)
         make_identity(nc, ident[:])
@@ -96,6 +119,7 @@ def tile_selfattention_pa_t_kernel(tc, q, k, v, out):
             bank = psum_bank("s%d" % a, [P, BLOCKS, P])
             blocks = [words_of(k_rows[a][:])[:, j * P : (j + 1) * P] for j in range(BLOCKS)]
             transpose_blocks(nc, bank, blocks, ident)
+            stay_warm(N_KEYS // 2, "o")
             copy = nc.scalar.copy if a % 2 == 0 else nc.vector.tensor_copy
             copy(
                 out=k_words[:, :, a * P : (a + 1) * P, :],
@@ -116,35 +140,40 @@ def tile_selfattention_pa_t_kernel(tc, q, k, v, out):
         w_banks, w_grps, w_codes, w_scales = {}, {}, {}, {}
         o_banks = {}
 
-        def transpose_queries(r):
-            for i in range(PAIR):
-                n = r * PAIR + i
-                row_words = words_of(q_pairs[r][:, i, :])
-                bank = psum_bank(("w", "o")[i] if r == 1 else "t%d" % i, [P, BLOCKS, P])
-                blocks = [row_words[:, j * P : (j + 1) * P] for j in range(BLOCKS)]
-                transpose_blocks(nc, bank, blocks, ident)
-                t_banks[n] = bank
+        def transpose_queries(r, i):
+            row_words = words_of(q_tiles[r * PAIR + i])
+            bank = psum_bank(("w", "o")[i] if r in (1, 3) else "t%d" % i, [P, BLOCKS, P])
+            blocks = [row_words[:, j * P : (j + 1) * P] for j in range(BLOCKS)]
+            transpose_blocks(nc, bank, blocks, ident)
+            t_banks[r, i] = bank
 
-        def group_queries(r):
-            q_grp = work.tile([P, PAIR * D_FEAT], BF16, align_bytes=64)
-            for i in range(PAIR):
-                tile_words = words_of(q_grp[:])[:, i * BLOCKS * P : (i + 1) * BLOCKS * P]
-                copy_interleaved(nc.scalar.copy, tile_words, t_banks[r * PAIR + i])
-            q_grps[r] = q_grp
+        def group_queries(r, i):
+            if i == 0:
+                q_grps[r] = work.tile([P, PAIR * D_FEAT], BF16, align_bytes=64, name="q_grp")
+            tile_words = words_of(q_grps[r][:])[:, i * BLOCKS * P : (i + 1) * BLOCKS * P]
+            copy_interleaved(nc.scalar.copy, tile_words, t_banks[r, i][:])
 
-        def quantise_queries(r):
-            q_code = work.tile([P, PAIR * FEAT_PASSES * P], U32, align_bytes=64)
-            q_scale = work.tile([P, PAIR * FEAT_PASSES * P], U8, align_bytes=64)
-            nc.vector.quantize_mx(out=q_code[:].bitcast(FP8X4), scales=q_scale[:], in_=q_grps[r][:])
+        def quantise_queries(r, calls=1):
+            width = PAIR * FEAT_PASSES * P
+            q_code = work.tile([P, width], U32, align_bytes=64)
+            q_scale = work.tile([P, width], U8, align_bytes=64)
+            for call in range(calls):
+                first, end = call * width // calls, (call + 1) * width // calls
+                nc.vector.quantize_mx(
+                    out=q_code[:, first:end].bitcast(FP8X4),
+                    scales=q_scale[:, first:end],
+                    in_=q_grps[r][:, first * PACK : end * PACK],
+                )
             q_codes[r], q_scales[r] = q_code, q_scale
 
         def scores(r):
             for i in range(PAIR):
-                s_bank = psum_bank("s%d" % ((r * PAIR + i) % 4), [P, N_KEYS])
+                s_banks[r, i] = psum_bank("s%d" % ((r * PAIR + i) % 4), [P, N_KEYS])
+            for i in range(PAIR):
                 for c in range(FEAT_PASSES):
                     cols = slice((i * FEAT_PASSES + c) * P, (i * FEAT_PASSES + c + 1) * P)
                     nc.tensor.matmul_mx(
-                        out=s_bank[:],
+                        out=s_banks[r, i][:],
                         lhsT=q_codes[r][:, cols].bitcast(FP8X4),
                         lhsT_scale=q_scales[r][:, cols],
                         rhs=k_codes[:, c, :].bitcast(FP8X4),
@@ -152,34 +181,38 @@ def tile_selfattention_pa_t_kernel(tc, q, k, v, out):
                         start=(c == 0),
                         stop=(c == FEAT_PASSES - 1),
                     )
-                s_banks[r * PAIR + i] = s_bank
 
-        def square_sums(r):
-            sumsq = work.tile([P, PAIR], F32)
-            for i in range(PAIR):
-                squares = work.tile([P, N_KEYS], BF16)
-                nc.scalar.activation(
-                    out=squares[:],
-                    in_=s_banks[r * PAIR + i][:],
-                    func=ACT.Square,
-                    accum_out=sumsq[:, i : i + 1],
-                )
-            sumsqs[r] = sumsq
-
-        def inverse_norms(r):
-            floored = work.tile([P, PAIR], F32)
-            nc.gpsimd.tensor_scalar(
-                out=floored[:], in0=sumsqs[r][:], scalar1=EPS * EPS, scalar2=None, op0=ALU.max
+        def square_sum(r, i):
+            if i == 0:
+                sumsqs[r] = work.tile([P, PAIR], F32, name="sumsq")
+            squares = work.tile([P, N_KEYS], BF16)
+            nc.scalar.activation(
+                out=squares[:],
+                in_=s_banks[r, i][:],
+                func=ACT.Square,
+                accum_out=sumsqs[r][:, i : i + 1],
             )
-            inverse = work.tile([P, PAIR], F32)
-            nc.gpsimd.tensor_tensor(out=inverse[:], in0=floored[:], in1=minus_half[:], op=ALU.pow)
-            inverses[r] = inverse
+
+        def inverse_norms(r, i=0, n=PAIR):
+            floored = work.tile([P, n], F32, name="floored%d" % n)
+            nc.gpsimd.tensor_scalar(
+                out=floored[:],
+                in0=sumsqs[r][:, i : i + n],
+                scalar1=EPS * EPS,
+                scalar2=None,
+                op0=ALU.max,
+            )
+            inverse = work.tile([P, n], F32, name="inverse%d" % n)
+            nc.gpsimd.tensor_tensor(
+                out=inverse[:], in0=floored[:], in1=minus_half[:, :n], op=ALU.pow
+            )
+            for j in range(n):
+                inverses[r, i + j] = inverse[:, j : j + 1]
 
         def scale_scores(r, i, on_scalar=False):
             if i == 0:
                 w_rows[r] = work.tile([P, PAIR, N_KEYS], BF16, name="w_row")
-            w_row, s_bank = w_rows[r][:, i, :], s_banks[r * PAIR + i][:]
-            inverse = inverses[r][:, i : i + 1]
+            w_row, s_bank, inverse = w_rows[r][:, i, :], s_banks[r, i][:], inverses[r, i]
             if on_scalar:
                 nc.scalar.activation(out=w_row, in_=s_bank, func=ACT.Copy, scale=inverse)
             else:
@@ -187,107 +220,145 @@ def tile_selfattention_pa_t_kernel(tc, q, k, v, out):
                     out=w_row, in0=s_bank, scalar1=inverse, scalar2=None, op0=ALU.mult
                 )
 
-        def transpose_weights(r):
-            w_bank = psum_bank("w" if r < DRAIN - 3 else ("t0", "t1", "w")[r % 3], [P, BLOCKS, P])
+        def transpose_weights(r, tag, i=0, n=PAIR):
+            w_banks[r, i] = psum_bank(tag, [P, BLOCKS, P])[:, : 2 * n, :]
             blocks = [
-                words_of(w_rows[r][:, i, :])[:, u * P : (u + 1) * P]
-                for i in range(PAIR)
+                words_of(w_rows[r][:, i + j, :])[:, u * P : (u + 1) * P]
+                for j in range(n)
                 for u in range(2)
             ]
-            transpose_blocks(nc, w_bank, blocks, ident)
-            w_banks[r] = w_bank
+            transpose_blocks(nc, w_banks[r, i], blocks, ident)
 
-        def group_weights(r, copy):
-            w_grp = work.tile([P, PAIR * N_KEYS], BF16, align_bytes=64)
-            copy_interleaved(copy, words_of(w_grp[:]), w_banks[r])
-            w_grps[r] = w_grp
+        def group_weights(r, copy, i=0, n=PAIR):
+            w_grps[r, i] = work.tile([P, n * N_KEYS], BF16, align_bytes=64, name="w_grp%d" % n)
+            copy_interleaved(copy, words_of(w_grps[r, i][:]), w_banks[r, i])
 
-        def quantise_weights(r):
-            w_code = work.tile([P, PAIR * P], U32, align_bytes=64)
-            w_scale = work.tile([P, PAIR * P], U8, align_bytes=64)
-            nc.vector.quantize_mx(out=w_code[:].bitcast(FP8X4), scales=w_scale[:], in_=w_grps[r][:])
-            w_codes[r], w_scales[r] = w_code, w_scale
+        def quantise_weights(r, i=0, n=PAIR):
+            w_code = work.tile([P, n * P], U32, align_bytes=64, name="w_code%d" % n)
+            w_scale = work.tile([P, n * P], U8, align_bytes=64, name="w_scale%d" % n)
+            nc.vector.quantize_mx(
+                out=w_code[:].bitcast(FP8X4), scales=w_scale[:], in_=w_grps[r, i][:]
+            )
+            w_codes[r, i], w_scales[r, i] = w_code, w_scale
 
-        def attend(r):
-            o_bank = psum_bank("o" if r < DRAIN - 2 else ("o", "s0", "s1")[r % 3], [P, PAIR, D_VAL])
-            for i in range(PAIR):
-                cols = slice(i * P, (i + 1) * P)
+        def attend(r, tag, i=0, n=PAIR):
+            o_banks[r, i] = psum_bank(tag, [P, PAIR, D_VAL])[:, :n, :]
+            for j in range(n):
+                cols = slice(j * P, (j + 1) * P)
                 nc.tensor.matmul_mx(
-                    out=o_bank[:, i, :],
-                    lhsT=w_codes[r][:, cols].bitcast(FP8X4),
-                    lhsT_scale=w_scales[r][:, cols],
+                    out=o_banks[r, i][:, j, :],
+                    lhsT=w_codes[r, i][:, cols].bitcast(FP8X4),
+                    lhsT_scale=w_scales[r, i][:, cols],
                     rhs=v_codes[:].bitcast(FP8X4),
                     rhs_scale=v_scales[:],
                     start=True,
                     stop=True,
                 )
-            o_banks[r] = o_bank
+
+        def leave(r, copy, i=0, n=PAIR):
+            first = r * PAIR + i
+            o_rows = o_pool.tile([P, n, D_VAL], F32, name="o_rows%d" % n)
+            copy(out=o_rows[:], in_=o_banks[r, i])
+            nc.sync.dma_start(out=out_rows[:, first : first + n, :], in_=o_rows[:])
 
         def leaves_on_vector(r):
             return r % VECTOR_LEAVE_EVERY == 0 and r < DRAIN - 2
 
-        def leave(r):
-            o_pair = o_pool.tile([P, PAIR, D_VAL], F32)
-            copy = nc.vector.tensor_copy if leaves_on_vector(r) else nc.scalar.copy
-            copy(out=o_pair[:], in_=o_banks[r][:])
-            nc.sync.dma_start(out=out_rows[:, r * PAIR : (r + 1) * PAIR, :], in_=o_pair[:])
-
-        transpose_queries(0)
-        transpose_queries(1)
-        group_queries(0)
-        group_queries(1)
-        quantise_queries(0)
+        def quantise_values():
+            nc.vector.tensor_copy(
+                out=v_grp[:].rearrange("p c (u e) -> p c u e", e=2),
+                in_=v_raw[:].rearrange("p u (e c) -> p c u e", e=2),
+            )
+            nc.vector.quantize_mx(
+                out=v_codes[:].bitcast(FP8X4),
+                scales=v_scales[:],
+                in_=v_grp[:].rearrange("p c t -> p (c t)"),
+            )
 
         v_codes = consts.tile([P, D_VAL], U32, align_bytes=64)
         v_scales = consts.tile([P, D_VAL], U8, align_bytes=64)
         v_grp = consts.tile([P, D_VAL, PACK], BF16, align_bytes=64)
 
+        for r in range(2):
+            for i in range(PAIR):
+                transpose_queries(r, i)
+                stay_warm(3 * P, "o" if (r, i) != (1, 1) else "s0")
+        for r in range(2):
+            for i in range(PAIR):
+                group_queries(r, i)
+        quantise_queries(0, calls=PAIR)
+
         def live(r):
             return 0 <= r < ROUNDS
 
-        for r in range(ROUNDS + 4):
+        scalar_copy, vector_copy = nc.scalar.copy, nc.vector.tensor_copy
+        for r in range(ROUNDS):
             if live(r - 5) and leaves_on_vector(r - 5):
-                leave(r - 5)
+                leave(r - 5, vector_copy)
 
+            if r == 0:
+                scores(r)
+                for i in range(PAIR):
+                    square_sum(r, i)
             if live(r + 2):
-                transpose_queries(r + 2)
+                for i in range(PAIR):
+                    transpose_queries(r + 2, i)
             if live(r - 3):
-                transpose_weights(r - 3)
-            if live(r):
+                transpose_weights(r - 3, {DRAIN: "t0", DRAIN + 1: "t1"}.get(r, "w"))
+            if r > 0:
                 scores(r)
             if live(r - 4):
-                attend(r - 4)
+                attend(r - 4, "o")
 
             if live(r + 2):
-                group_queries(r + 2)
+                for i in range(PAIR):
+                    group_queries(r + 2, i)
             if r == DRAIN:
-                group_weights(r - 3, nc.scalar.copy)
-            if live(r):
-                square_sums(r)
-            if r == ROUNDS:
-                scale_scores(r - 1, 0, on_scalar=True)
+                group_weights(r - 3, scalar_copy)
+            if r > 0:
+                for i in range(PAIR):
+                    square_sum(r, i)
+                    if r == LAST:
+                        inverse_norms(r, i, 1)
             if live(r - 4) and not leaves_on_vector(r - 4):
-                leave(r - 4)
-
-            if live(r):
+                leave(r - 4, scalar_copy)
+            if r < LAST:
                 inverse_norms(r)
 
-            if live(r + 1):
+            if 0 < r + 1 < ROUNDS:
                 quantise_queries(r + 1)
             if live(r - 3) and r != DRAIN:
-                group_weights(r - 3, nc.vector.tensor_copy)
+                group_weights(r - 3, vector_copy)
             if live(r - 1):
-                for i in range(PAIR) if r < ROUNDS else (1,):
+                for i in range(PAIR):
                     scale_scores(r - 1, i)
             if r == 1:
-                nc.vector.tensor_copy(
-                    out=v_grp[:].rearrange("p c (u e) -> p c u e", e=2),
-                    in_=v_raw[:].rearrange("p u (e c) -> p c u e", e=2),
-                )
-                nc.vector.quantize_mx(
-                    out=v_codes[:].bitcast(FP8X4),
-                    scales=v_scales[:],
-                    in_=v_grp[:].rearrange("p c t -> p (c t)"),
-                )
+                quantise_values()
             if live(r - 3):
                 quantise_weights(r - 3)
+
+        transpose_weights(LAST - 2, "w")
+        attend(LAST - 3, "s1")
+        group_weights(LAST - 2, vector_copy)
+        quantise_weights(LAST - 2)
+        for i in range(PAIR):
+            scale_scores(LAST, i, on_scalar=(i == 0))
+        transpose_weights(LAST, "s0", 0, 1)
+        transpose_weights(LAST - 1, "t0")
+        group_weights(LAST, scalar_copy, 0, 1)
+        leave(LAST - 3, scalar_copy)
+        group_weights(LAST - 1, vector_copy)
+        quantise_weights(LAST, 0, 1)
+        quantise_weights(LAST - 1)
+
+        transpose_weights(LAST, "s1", 1, 1)
+        attend(LAST - 2, "t1")
+        attend(LAST, "s2", 0, 1)
+        attend(LAST - 1, "o")
+        leave(LAST - 2, scalar_copy)
+        leave(LAST, scalar_copy, 0, 1)
+        leave(LAST - 1, scalar_copy)
+        group_weights(LAST, vector_copy, 1, 1)
+        quantise_weights(LAST, 1, 1)
+        attend(LAST, "s3", 1, 1)
+        leave(LAST, vector_copy, 1, 1)

@@ -23,7 +23,7 @@ Q_TILES = N_QUERIES // P
 PAIR = 2
 ROUNDS = Q_TILES // PAIR
 DRAIN = ROUNDS - PAIR
-VECTOR_LEAVE_EVERY = 4
+SCALAR_COLUMNS = 384
 LAST = ROUNDS - 1
 BLOCKS = 4
 
@@ -57,7 +57,7 @@ def tile_selfattention_pa_t_kernel(tc, q, k, v, out):
         consts = ctx.enter_context(tc.tile_pool(name="consts", bufs=1))
         q_pool = ctx.enter_context(tc.tile_pool(name="q_pool", bufs=ROUNDS))
         work = ctx.enter_context(tc.tile_pool(name="work", bufs=3))
-        o_pool = ctx.enter_context(tc.tile_pool(name="o_pool", bufs=8))
+        o_pool = ctx.enter_context(tc.tile_pool(name="o_pool", bufs=10))
         psum = ctx.enter_context(tc.psum_pool(name="psum", bufs=1))
 
         def psum_bank(tag, shape):
@@ -261,8 +261,22 @@ def tile_selfattention_pa_t_kernel(tc, q, k, v, out):
             copy(out=o_rows[:], in_=o_banks[r, i])
             nc.sync.dma_start(out=out_rows[:, first : first + n, :], in_=o_rows[:])
 
-        def leaves_on_vector(r):
-            return r % VECTOR_LEAVE_EVERY == 0 and r < DRAIN - 2
+        o_halves = {}
+
+        def leave_on_scalar(r):
+            o_halves[r] = o_pool.tile([P, PAIR * D_VAL], F32, name="o_rows2")
+            bank = o_banks[r, 0].rearrange("p i c -> p (i c)")
+            nc.scalar.copy(out=o_halves[r][:, :SCALAR_COLUMNS], in_=bank[:, :SCALAR_COLUMNS])
+
+        def leave_on_vector(r):
+            bank = o_banks[r, 0].rearrange("p i c -> p (i c)")
+            nc.vector.tensor_copy(
+                out=o_halves[r][:, SCALAR_COLUMNS:], in_=bank[:, SCALAR_COLUMNS:]
+            )
+            nc.sync.dma_start(
+                out=out_rows[:, r * PAIR : (r + 1) * PAIR, :],
+                in_=o_halves[r][:].rearrange("p (i c) -> p i c", i=PAIR),
+            )
 
         def quantise_values():
             nc.vector.tensor_copy(
@@ -293,8 +307,8 @@ def tile_selfattention_pa_t_kernel(tc, q, k, v, out):
 
         scalar_copy, vector_copy = nc.scalar.copy, nc.vector.tensor_copy
         for r in range(ROUNDS):
-            if live(r - 5) and leaves_on_vector(r - 5):
-                leave(r - 5, vector_copy)
+            if live(r - 5):
+                leave_on_vector(r - 5)
 
             if r == 0:
                 scores(r)
@@ -320,8 +334,11 @@ def tile_selfattention_pa_t_kernel(tc, q, k, v, out):
                     square_sum(r, i)
                     if r == LAST:
                         inverse_norms(r, i, 1)
-            if live(r - 4) and not leaves_on_vector(r - 4):
-                leave(r - 4, scalar_copy)
+            if live(r - 4):
+                if r < LAST:
+                    leave_on_scalar(r - 4)
+                else:
+                    leave(r - 4, scalar_copy)
             if r < LAST:
                 inverse_norms(r)
 

@@ -23,7 +23,7 @@ Q_TILES = N_QUERIES // P
 PAIR = 2
 ROUNDS = Q_TILES // PAIR
 DRAIN = ROUNDS - PAIR
-SCALAR_COLUMNS = 384
+SCALAR_COLUMNS = 400
 LAST = ROUNDS - 1
 BLOCKS = 4
 
@@ -147,11 +147,11 @@ def tile_selfattention_pa_t_kernel(tc, q, k, v, out):
             transpose_blocks(nc, bank, blocks, ident)
             t_banks[r, i] = bank
 
-        def group_queries(r, i):
+        def group_queries(r, i, copy=nc.scalar.copy):
             if i == 0:
                 q_grps[r] = work.tile([P, PAIR * D_FEAT], BF16, align_bytes=64, name="q_grp")
             tile_words = words_of(q_grps[r][:])[:, i * BLOCKS * P : (i + 1) * BLOCKS * P]
-            copy_interleaved(nc.scalar.copy, tile_words, t_banks[r, i][:])
+            copy_interleaved(copy, tile_words, t_banks[r, i][:])
 
         def quantise_queries(r, calls=1):
             width = PAIR * FEAT_PASSES * P
@@ -325,8 +325,11 @@ def tile_selfattention_pa_t_kernel(tc, q, k, v, out):
                 attend(r - 4, "o")
 
             if live(r + 2):
-                for i in range(PAIR):
-                    group_queries(r + 2, i)
+                group_queries(r + 2, 0)
+            if r == DRAIN - 1:
+                group_weights(r - 3, scalar_copy)
+            if live(r + 2):
+                group_queries(r + 2, 1, vector_copy if r == 1 else scalar_copy)
             if r == DRAIN:
                 group_weights(r - 3, scalar_copy)
             if r > 0:
@@ -344,13 +347,13 @@ def tile_selfattention_pa_t_kernel(tc, q, k, v, out):
 
             if 0 < r + 1 < ROUNDS:
                 quantise_queries(r + 1)
-            if live(r - 3) and r != DRAIN:
+            if r == 0:
+                quantise_values()
+            if live(r - 3) and r not in (DRAIN - 1, DRAIN):
                 group_weights(r - 3, vector_copy)
             if live(r - 1):
                 for i in range(PAIR):
                     scale_scores(r - 1, i)
-            if r == 1:
-                quantise_values()
             if live(r - 3):
                 quantise_weights(r - 3)
 
@@ -362,8 +365,8 @@ def tile_selfattention_pa_t_kernel(tc, q, k, v, out):
             scale_scores(LAST, i, on_scalar=(i == 0))
         transpose_weights(LAST, "s0", 0, 1)
         transpose_weights(LAST - 1, "t0")
-        group_weights(LAST, scalar_copy, 0, 1)
         leave(LAST - 3, scalar_copy)
+        group_weights(LAST, scalar_copy, 0, 1)
         group_weights(LAST - 1, vector_copy)
         quantise_weights(LAST, 0, 1)
         quantise_weights(LAST - 1)

from contextlib import ExitStack

import concourse.mybir as mybir
from concourse.masks import make_identity

F32 = mybir.dt.float32
BF16 = mybir.dt.bfloat16
U32 = mybir.dt.uint32
U8 = mybir.dt.uint8
FP8X4 = mybir.dt.float8_e4m3fn_x4
ACT = mybir.ActivationFunctionType
ALU = mybir.AluOpType

N_QUERIES, N_KEYS, D_FEAT, D_VAL = 8192, 512, 1024, 256
EPS = 1e-12

P = 128
PACK = 4
K_PASS = P * PACK
FEAT_PASSES = D_FEAT // K_PASS
KEY_TILES = N_KEYS // P
Q_TILES = N_QUERIES // P
PAIR = 2
ROUNDS = Q_TILES // PAIR
DRAIN = ROUNDS - PAIR
SCALAR_COLUMNS = 400
LAST = ROUNDS - 1
BLOCKS = 4

FLOPS = 2 * N_QUERIES * N_KEYS * (D_FEAT + D_VAL)


def words_of(rows_bf16):
    return rows_bf16.bitcast(F32)


def transpose_blocks(nc, bank, blocks, ident):
    for j, block in enumerate(blocks):
        nc.tensor.transpose(bank[:, j, :], block, ident[:])


def copy_interleaved(copy, grouped_words, bank):
    copy(
        out=grouped_words.rearrange("p (a r u) -> p a r u", r=P, u=2),
        in_=bank.rearrange("p (a u) r -> p a r u", u=2),
    )


def tile_selfattention_pa_t_kernel(tc, q, k, v, out):
    nc = tc.nc
    q_rows = q.rearrange("(p n) d -> p n d", n=Q_TILES)
    out_rows = out.rearrange("(p n) c -> p n c", n=Q_TILES)

    with ExitStack() as ctx:
        ctx.enter_context(tc.manual_schedule())

        consts = ctx.enter_context(tc.tile_pool(name="consts", bufs=1))
        q_pool = ctx.enter_context(tc.tile_pool(name="q_pool", bufs=ROUNDS))
        work = ctx.enter_context(tc.tile_pool(name="work", bufs=3))
        o_pool = ctx.enter_context(tc.tile_pool(name="o_pool", bufs=10))
        psum = ctx.enter_context(tc.psum_pool(name="psum", bufs=1))

        def psum_bank(tag, shape):
            return psum.tile(shape, F32, name="bank_" + tag)

        q_tiles = []

        def load_pair(r, loads=1):
            q_pair = q_pool.tile([P, PAIR, D_FEAT], BF16)
            size = PAIR // loads
            for i in range(0, PAIR, size):
                first = r * PAIR + i
                nc.sync.dma_start(
                    out=q_pair[:, i : i + size, :], in_=q_rows[:, first : first + size, :]
                )
            q_tiles.extend([q_pair[:, i, :] for i in range(PAIR)])

        k_tiled = k.rearrange("(a p) d -> p a d", p=P)
        k_rows = []
        for a in range(KEY_TILES):
            k_row = consts.tile([P, D_FEAT], BF16, name="k_row%d" % a)
            nc.sync.dma_start(out=k_row[:], in_=k_tiled[:, a, :])
            k_rows.append(k_row)
        load_pair(0, loads=PAIR)
        load_pair(1)
        load_pair(2)
        v_raw = consts.tile([P, 2, 2 * D_VAL], BF16)
        nc.sync.dma_start(out=v_raw[:], in_=v.rearrange("(u p e) c -> p u (e c)", u=2, e=2))
        for r in range(3, ROUNDS):
            load_pair(r)

        zeros = consts.tile([P, N_KEYS], BF16)
        nc.vector.memset(zeros[:], 0.0)

        def stay_warm(columns, tag):
            bank = psum_bank(tag, [P, N_KEYS])
            nc.tensor.matmul(
                out=bank[:, :columns],
                lhsT=zeros[:, :P],
                rhs=zeros[:, :columns],
                start=True,
                stop=True,
            )

        for step in range(4):
            stay_warm(N_KEYS, "o")

        ident = consts.tile([P, P], F32)
        make_identity(nc, ident[:])

        minus_half = consts.tile([P, PAIR], F32)
        nc.vector.memset(minus_half[:], -0.5)

        k_grp = consts.tile([P, FEAT_PASSES * N_KEYS * PACK], BF16, align_bytes=64)
        k_codes = consts.tile([P, FEAT_PASSES, N_KEYS], U32, align_bytes=64)
        k_scales = consts.tile([P, FEAT_PASSES, N_KEYS], U8, align_bytes=64)
        k_words = words_of(k_grp[:]).rearrange("p (c k u) -> p c k u", c=FEAT_PASSES, u=2)
        for a in range(KEY_TILES):
            bank = psum_bank("s%d" % a, [P, BLOCKS, P])
            blocks = [words_of(k_rows[a][:])[:, j * P : (j + 1) * P] for j in range(BLOCKS)]
            transpose_blocks(nc, bank, blocks, ident)
            stay_warm(N_KEYS // 2, "o")
            copy = nc.scalar.copy if a % 2 == 0 else nc.vector.tensor_copy
            copy(
                out=k_words[:, :, a * P : (a + 1) * P, :],
                in_=bank[:].rearrange("p (c u) r -> p c r u", u=2),
            )
        for half in range(2):
            for c in range(FEAT_PASSES):
                keys = slice(half * 2 * P, (half + 1) * 2 * P)
                first = (c * N_KEYS + half * 2 * P) * PACK
                nc.vector.quantize_mx(
                    out=k_codes[:, c, keys].bitcast(FP8X4),
                    scales=k_scales[:, c, keys],
                    in_=k_grp[:, first : first + 2 * P * PACK],
                )

        t_banks, q_grps, q_codes, q_scales = {}, {}, {}, {}
        s_banks, sumsqs, inverses, w_rows = {}, {}, {}, {}
        w_banks, w_grps, w_codes, w_scales = {}, {}, {}, {}
        o_banks = {}

        def transpose_queries(r, i):
            row_words = words_of(q_tiles[r * PAIR + i])
            bank = psum_bank(("w", "o")[i] if r in (1, 3) else "t%d" % i, [P, BLOCKS, P])
            blocks = [row_words[:, j * P : (j + 1) * P] for j in range(BLOCKS)]
            transpose_blocks(nc, bank, blocks, ident)
            t_banks[r, i] = bank

        def group_queries(r, i, copy=nc.scalar.copy):
            if i == 0:
                q_grps[r] = work.tile([P, PAIR * D_FEAT], BF16, align_bytes=64, name="q_grp")
            tile_words = words_of(q_grps[r][:])[:, i * BLOCKS * P : (i + 1) * BLOCKS * P]
            copy_interleaved(copy, tile_words, t_banks[r, i][:])

        def quantise_queries(r, calls=1):
            width = PAIR * FEAT_PASSES * P
            q_code = work.tile([P, width], U32, align_bytes=64)
            q_scale = work.tile([P, width], U8, align_bytes=64)
            for call in range(calls):
                first, end = call * width // calls, (call + 1) * width // calls
                nc.vector.quantize_mx(
                    out=q_code[:, first:end].bitcast(FP8X4),
                    scales=q_scale[:, first:end],
                    in_=q_grps[r][:, first * PACK : end * PACK],
                )
            q_codes[r], q_scales[r] = q_code, q_scale

        def scores(r):
            for i in range(PAIR):
                s_banks[r, i] = psum_bank("s%d" % ((r * PAIR + i) % 4), [P, N_KEYS])
            for i in range(PAIR):
                for c in range(FEAT_PASSES):
                    cols = slice((i * FEAT_PASSES + c) * P, (i * FEAT_PASSES + c + 1) * P)
                    nc.tensor.matmul_mx(
                        out=s_banks[r, i][:],
                        lhsT=q_codes[r][:, cols].bitcast(FP8X4),
                        lhsT_scale=q_scales[r][:, cols],
                        rhs=k_codes[:, c, :].bitcast(FP8X4),
                        rhs_scale=k_scales[:, c, :],
                        start=(c == 0),
                        stop=(c == FEAT_PASSES - 1),
                    )

        def square_sum(r, i):
            if i == 0:
                sumsqs[r] = work.tile([P, PAIR], F32, name="sumsq")
            squares = work.tile([P, N_KEYS], BF16)
            nc.scalar.activation(
                out=squares[:],
                in_=s_banks[r, i][:],
                func=ACT.Square,
                accum_out=sumsqs[r][:, i : i + 1],
            )

        def inverse_norms(r, i=0, n=PAIR):
            floored = work.tile([P, n], F32, name="floored%d" % n)
            nc.gpsimd.tensor_scalar(
                out=floored[:],
                in0=sumsqs[r][:, i : i + n],
                scalar1=EPS * EPS,
                scalar2=None,
                op0=ALU.max,
            )
            inverse = work.tile([P, n], F32, name="inverse%d" % n)
            nc.gpsimd.tensor_tensor(
                out=inverse[:], in0=floored[:], in1=minus_half[:, :n], op=ALU.pow
            )
            for j in range(n):
                inverses[r, i + j] = inverse[:, j : j + 1]

        def scale_scores(r, i, on_scalar=False):
            if i == 0:
                w_rows[r] = work.tile([P, PAIR, N_KEYS], BF16, name="w_row")
            w_row, s_bank, inverse = w_rows[r][:, i, :], s_banks[r, i][:], inverses[r, i]
            if on_scalar:
                nc.scalar.activation(out=w_row, in_=s_bank, func=ACT.Copy, scale=inverse)
            else:
                nc.vector.tensor_scalar(
                    out=w_row, in0=s_bank, scalar1=inverse, scalar2=None, op0=ALU.mult
                )

        def transpose_weights(r, tag, i=0, n=PAIR):
            w_banks[r, i] = psum_bank(tag, [P, BLOCKS, P])[:, : 2 * n, :]
            blocks = [
                words_of(w_rows[r][:, i + j, :])[:, u * P : (u + 1) * P]
                for j in range(n)
                for u in range(2)
            ]
            transpose_blocks(nc, w_banks[r, i], blocks, ident)

        def group_weights(r, copy, i=0, n=PAIR):
            w_grps[r, i] = work.tile([P, n * N_KEYS], BF16, align_bytes=64, name="w_grp%d" % n)
            copy_interleaved(copy, words_of(w_grps[r, i][:]), w_banks[r, i])

        def quantise_weights(r, i=0, n=PAIR):
            w_code = work.tile([P, n * P], U32, align_bytes=64, name="w_code%d" % n)
            w_scale = work.tile([P, n * P], U8, align_bytes=64, name="w_scale%d" % n)
            nc.vector.quantize_mx(
                out=w_code[:].bitcast(FP8X4), scales=w_scale[:], in_=w_grps[r, i][:]
            )
            w_codes[r, i], w_scales[r, i] = w_code, w_scale

        def attend(r, tag, i=0, n=PAIR):
            o_banks[r, i] = psum_bank(tag, [P, PAIR, D_VAL])[:, :n, :]
            for j in range(n):
                cols = slice(j * P, (j + 1) * P)
                nc.tensor.matmul_mx(
                    out=o_banks[r, i][:, j, :],
                    lhsT=w_codes[r, i][:, cols].bitcast(FP8X4),
                    lhsT_scale=w_scales[r, i][:, cols],
                    rhs=v_codes[:].bitcast(FP8X4),
                    rhs_scale=v_scales[:],
                    start=True,
                    stop=True,
                )

        def leave(r, copy, i=0, n=PAIR):
            first = r * PAIR + i
            o_rows = o_pool.tile([P, n, D_VAL], F32, name="o_rows%d" % n)
            copy(out=o_rows[:], in_=o_banks[r, i])
            nc.sync.dma_start(out=out_rows[:, first : first + n, :], in_=o_rows[:])

        o_halves = {}

        def leave_on_scalar(r):
            o_halves[r] = o_pool.tile([P, PAIR * D_VAL], F32, name="o_rows2")
            bank = o_banks[r, 0].rearrange("p i c -> p (i c)")
            nc.scalar.copy(out=o_halves[r][:, :SCALAR_COLUMNS], in_=bank[:, :SCALAR_COLUMNS])

        def leave_on_vector(r):
            bank = o_banks[r, 0].rearrange("p i c -> p (i c)")
            nc.vector.tensor_copy(
                out=o_halves[r][:, SCALAR_COLUMNS:], in_=bank[:, SCALAR_COLUMNS:]
            )
            nc.sync.dma_start(
                out=out_rows[:, r * PAIR : (r + 1) * PAIR, :],
                in_=o_halves[r][:].rearrange("p (i c) -> p i c", i=PAIR),
            )

        def quantise_values():
            nc.vector.tensor_copy(
                out=v_grp[:].rearrange("p c (u e) -> p c u e", e=2),
                in_=v_raw[:].rearrange("p u (e c) -> p c u e", e=2),
            )
            nc.vector.quantize_mx(
                out=v_codes[:].bitcast(FP8X4),
                scales=v_scales[:],
                in_=v_grp[:].rearrange("p c t -> p (c t)"),
            )

        v_codes = consts.tile([P, D_VAL], U32, align_bytes=64)
        v_scales = consts.tile([P, D_VAL], U8, align_bytes=64)
        v_grp = consts.tile([P, D_VAL, PACK], BF16, align_bytes=64)

        for r in range(2):
            for i in range(PAIR):
                transpose_queries(r, i)
                stay_warm(3 * P, "o" if (r, i) != (1, 1) else "s0")
        for r in range(2):
            for i in range(PAIR):
                group_queries(r, i)
        quantise_queries(0, calls=PAIR)

        def live(r):
            return 0 <= r < ROUNDS

        scalar_copy, vector_copy = nc.scalar.copy, nc.vector.tensor_copy
        for r in range(ROUNDS):
            if live(r - 5):
                leave_on_vector(r - 5)

            if r == 0:
                scores(r)
                for i in range(PAIR):
                    square_sum(r, i)
            if live(r + 2):
                for i in range(PAIR):
                    transpose_queries(r + 2, i)
            if live(r - 3):
                transpose_weights(r - 3, {DRAIN: "t0", DRAIN + 1: "t1"}.get(r, "w"))
            if r > 0:
                scores(r)
            if live(r - 4):
                attend(r - 4, "o")

            if live(r + 2):
                group_queries(r + 2, 0)
            if r == DRAIN - 1:
                group_weights(r - 3, scalar_copy)
            if live(r + 2):
                group_queries(r + 2, 1, vector_copy if r == 1 else scalar_copy)
            if r == DRAIN:
                group_weights(r - 3, scalar_copy)
            if r > 0:
                for i in range(PAIR):
                    square_sum(r, i)
                    if r == LAST:
                        inverse_norms(r, i, 1)
            if live(r - 4):
                if r < LAST:
                    leave_on_scalar(r - 4)
                else:
                    leave(r - 4, scalar_copy)
            if r < LAST:
                inverse_norms(r)

            if 0 < r + 1 < ROUNDS:
                quantise_queries(r + 1)
            if r == 0:
                quantise_values()
            if live(r - 3) and r not in (DRAIN - 1, DRAIN):
                group_weights(r - 3, vector_copy)
            if live(r - 1):
                for i in range(PAIR):
                    scale_scores(r - 1, i)
            if live(r - 3):
                quantise_weights(r - 3)

        transpose_weights(LAST - 2, "w")
        attend(LAST - 3, "s1")
        group_weights(LAST - 2, vector_copy)
        quantise_weights(LAST - 2)
        for i in range(PAIR):
            scale_scores(LAST, i, on_scalar=(i == 0))
        transpose_weights(LAST, "s0", 0, 1)
        transpose_weights(LAST - 1, "t0")
        leave(LAST - 3, scalar_copy)
        group_weights(LAST, scalar_copy, 0, 1)
        group_weights(LAST - 1, vector_copy)
        quantise_weights(LAST, 0, 1)
        quantise_weights(LAST - 1)

        transpose_weights(LAST, "s1", 1, 1)
        attend(LAST - 2, "t1")
        attend(LAST, "s2", 0, 1)
        attend(LAST - 1, "o")
        leave(LAST - 2, scalar_copy)
        leave(LAST, scalar_copy, 0, 1)
        leave(LAST - 1, scalar_copy)
        group_weights(LAST, vector_copy, 1, 1)
        quantise_weights(LAST, 1, 1)
        attend(LAST, "s3", 1, 1)
        leave(LAST, vector_copy, 1, 1)
